import numpy as np
import ml_dtypes


def mxq(x, axis, fmt="e4m3"):
    dtype, down = {"e4m3": (ml_dtypes.float8_e4m3fn, 7), "e5m2": (ml_dtypes.float8_e5m2, 14)}[fmt]
    v = np.moveaxis(np.asarray(x, np.float32).astype(ml_dtypes.bfloat16).astype(np.float64), axis, -1)
    blocks = v.reshape(v.shape[:-1] + (-1, 32))
    amax = np.abs(blocks).max(-1, keepdims=True)
    byte = np.maximum(np.where(amax > 0, np.frexp(amax)[1] - 1 + 127, 0) - down, 1)
    scale = np.exp2(byte - 127.0)
    codes = (blocks / scale).astype(np.float32).astype(dtype).astype(np.float64)
    return np.moveaxis((codes * scale).reshape(v.shape), -1, axis)


WIDE = False


def mx_kscale(k):
    if not WIDE:
        return np.ones(k)
    levels = np.array([10, -10, 5, -5, 0])
    a = np.random.permutation(np.resize(levels, k // 512 * 4)).reshape(k // 512, 4)
    idx = np.arange(k)
    return np.exp2(a[idx // 512, idx % 128 // 32])


BF16 = ml_dtypes.bfloat16


def bf(x):
    return np.asarray(x, np.float32).astype(BF16)


def f64(x):
    return np.asarray(x).astype(np.float64)


BS, N, D, B, D_PM = 2, 1024, 1024, 8, 512


def sigmoid(v):
    return 1.0 / (1.0 + np.exp(-v))


def setup_inputs():
    k = mx_kscale(D)
    m = 3.0 * np.random.rand(BS, N, 1)
    return {"H": bf(np.random.standard_normal((BS, N, D)) * k),
            "surprise": bf(np.random.standard_normal((BS, N, D)) * m),
            "proj_in_w": bf(np.random.standard_normal((D_PM, D)) / np.sqrt(D) / k),
            "proj_in_b": bf(np.random.standard_normal(D_PM) * 0.1),
            "surp_scale": bf((1.0 + 0.1 * np.random.standard_normal(1)) / np.sqrt(D)),
            "surp_bias": bf(-1.5 + 0.1 * np.random.standard_normal(1))}


def reference(H, surprise, proj_in_w, proj_in_b, surp_scale, surp_bias):
    pre = (mxq(f64(H), 2, "e4m3") @ mxq(f64(proj_in_w), 1, "e4m3").T) + f64(proj_in_b)
    surp_mag = np.sqrt(np.sum(f64(surprise) ** 2, axis=-1))
    s = sigmoid(f64(surp_scale) * surp_mag + f64(surp_bias))
    weighted = np.sqrt(s)[..., None] * pre
    wq = mxq(weighted, 1, "e4m3")
    return (wq.transpose(0, 2, 1) @ wq) / N

@@ -1,0 +1,293 @@
+from contextlib import ExitStack
+
+import concourse.mybir as mybir
+from concourse.masks import make_identity
+
+F32 = mybir.dt.float32
+BF16 = mybir.dt.bfloat16
+U32 = mybir.dt.uint32
+U8 = mybir.dt.uint8
+FP8X4 = mybir.dt.float8_e4m3fn_x4
+ALU = mybir.AluOpType
+ACT = mybir.ActivationFunctionType
+
+P = 128
+SAMPLES, TOKENS, D, F = 2, 1024, 1024, 512
+PACK = 4
+GROUP = P * PACK
+GROUPS = SAMPLES * TOKENS // GROUP
+PASSES = D // (P * PACK)
+CHUNKS = F // P
+FLOPS = 2 * SAMPLES * TOKENS * D * F + 2 * SAMPLES * F * F * TOKENS
+
+W_CHUNKS_ON_VECTOR = (0, 2)
+SLICES_ON_VECTOR = ((2, 3), (0, 2), (0,), (0,))
+ROWS_BEFORE_SIGMOID = 2
+STORES_BEFORE_LAST_SIGMOID = 3
+
+GAIN_COL, BIAS_COL, CONST_COLS = 0, 16, 64
+
+
+def tile_proceduralmemory_pa_kernel(
+    tc, H, surprise, proj_in_w, proj_in_b, surp_scale, surp_bias, out
+):
+    nc = tc.nc
+    with ExitStack() as ctx:
+        ctx.enter_context(tc.manual_schedule())
+        const = ctx.enter_context(tc.tile_pool(name="const", bufs=1))
+        inputs = ctx.enter_context(tc.tile_pool(name="inputs", bufs=1))
+        rotate = ctx.enter_context(tc.tile_pool(name="rotate", bufs=2))
+        keep = ctx.enter_context(tc.tile_pool(name="keep", bufs=1))
+        results = ctx.enter_context(tc.tile_pool(name="results", bufs=CHUNKS))
+        psum = ctx.enter_context(tc.psum_pool(name="psum", bufs=1))
+
+        def bank(index, shape, name):
+            return psum.tile(shape, F32, name=name, tag="bank%d" % index)
+
+        gram_bank = CHUNKS
+
+        const_row = const.tile([P, F + CONST_COLS], BF16, name="const_row")
+        nc.vector.memset(const_row[:], 0.0)
+        nc.scalar.dma_start(out=const_row[0:1, 0:F], in_=proj_in_b.unsqueeze(0))
+        nc.scalar.dma_start(
+            out=const_row[0:1, F + GAIN_COL : F + GAIN_COL + 1], in_=surp_scale.unsqueeze(0)
+        )
+        nc.scalar.dma_start(
+            out=const_row[0:1, F + BIAS_COL : F + BIAS_COL + 1], in_=surp_bias.unsqueeze(0)
+        )
+        half = const.tile([P, PACK], F32, name="half")
+        nc.vector.memset(half[:], 0.5)
+        table_warm = const.tile([P, 1], F32, name="table_warm")
+        nc.scalar.activation(out=table_warm[:], in_=half[:, 0:1], func=ACT.Sigmoid)
+        ones = const.tile([P, P], BF16, name="ones")
+        nc.vector.memset(ones[:], 1.0)
+        identity = const.tile([P, P], F32, name="identity")
+        make_identity(nc, identity[:])
+
+        w_in = inputs.tile([P, CHUNKS, D], BF16, name="w_in")
+        w_view = proj_in_w.rearrange("(c p) d -> p c d", p=P)
+        h_view = H.rearrange("b (g p t) d -> (b g) p t d", p=P, t=PACK)
+        s_view = surprise.rearrange("b (g p t) d -> (b g) p t d", p=P, t=PACK)
+        h_in = [inputs.tile([P, PACK, D], BF16, name="h_in%d" % g) for g in range(GROUPS)]
+        s_in = [inputs.tile([P, PACK, D], BF16, name="s_in%d" % g) for g in range(GROUPS)]
+        for c in range(CHUNKS):
+            nc.sync.dma_start(out=w_in[:, c, :], in_=w_view[:, c, :])
+        for t in range(PACK):
+            nc.sync.dma_start(out=h_in[0][:, t, :], in_=h_view[0][:, t, :])
+        for t in range(PACK):
+            nc.sync.dma_start(out=s_in[0][:, t, :], in_=s_view[0][:, t, :])
+        for g in range(1, GROUPS):
+            nc.sync.dma_start(out=h_in[g][:], in_=h_view[g])
+            nc.sync.dma_start(out=s_in[g][:], in_=s_view[g])
+
+        bias_all = const.tile([P, F], F32, name="bias_all")
+        gate_consts = const.tile([P, CONST_COLS], F32, name="gate_consts")
+        w_grouped = keep.tile([P, PASSES * F * PACK], BF16, name="w_grouped", align_bytes=64)
+        w_grouped_pairs = w_grouped[:].bitcast(F32).rearrange(
+            "p (k f u) -> p k f u", k=PASSES, f=F, u=2
+        )
+        w_words = keep.tile([P, PASSES * F], U32, name="w_words", align_bytes=64)
+        w_scales = keep.tile([P, PASSES * F], U8, name="w_scales", align_bytes=64)
+
+        flipped = {}
+        h_grouped, h_words, h_scales = {}, {}, {}
+        pre_banks = {}
+        biased, weighted, weighted_words, weighted_scales = {}, {}, {}, {}
+        square_sums, gates = {}, {}
+        gram_banks = {}
+
+        def transpose_pairs(key, rows, index):
+            pairs = rows.bitcast(F32)
+            planes = bank(index, [P, 2 * PASSES, P], "flipped")
+            for j in range(2 * PASSES):
+                nc.tensor.transpose(planes[:, j, :], pairs[:, j * P : (j + 1) * P], identity[:])
+            flipped[key] = planes
+
+        def copy_out(key, grouped_pairs, on_vector):
+            alternating = flipped[key][:].rearrange("p (k u) r -> p k r u", u=2)
+            if on_vector:
+                nc.vector.tensor_copy(out=grouped_pairs, in_=alternating)
+            else:
+                nc.scalar.copy(out=grouped_pairs, in_=alternating)
+
+        def copy_out_slice(g, t):
+            if g not in h_grouped:
+                h_grouped[g] = rotate.tile(
+                    [P, PACK * PASSES * P * PACK], BF16, name="h_grouped", align_bytes=64
+                )
+            pairs = h_grouped[g][:].bitcast(F32).rearrange(
+                "p (t k r u) -> p t k r u", t=PACK, k=PASSES, r=P, u=2
+            )
+            copy_out((g, t), pairs[:, t], t in SLICES_ON_VECTOR[g])
+
+        slice_words = PASSES * P
+
+        def quantise_h(g, first):
+            if g not in h_words:
+                h_words[g] = rotate.tile([P, PACK * slice_words], U32, name="h_words", align_bytes=64)
+                h_scales[g] = rotate.tile(
+                    [P, PACK * slice_words], U8, name="h_scales", align_bytes=64
+                )
+            cols = slice(first * slice_words, (first + 2) * slice_words)
+            nc.vector.quantize_mx(
+                out=h_words[g][:, cols].bitcast(FP8X4),
+                scales=h_scales[g][:, cols],
+                in_=h_grouped[g][:, first * slice_words * PACK : (first + 2) * slice_words * PACK],
+            )
+
+        def project(g, first):
+            for t in (first, first + 1):
+                for c in range(CHUNKS):
+                    if (g, c) not in pre_banks:
+                        pre_banks[(g, c)] = bank(c, [P, PACK, P], "pre")
+                    for k in range(PASSES):
+                        tokens = slice(t * slice_words + k * P, t * slice_words + (k + 1) * P)
+                        features = slice(k * F + c * P, k * F + (c + 1) * P)
+                        nc.tensor.matmul_mx(
+                            out=pre_banks[(g, c)][:, t, :],
+                            lhsT=h_words[g][:, tokens].bitcast(FP8X4),
+                            lhsT_scale=h_scales[g][:, tokens],
+                            rhs=w_words[:, features].bitcast(FP8X4),
+                            rhs_scale=w_scales[:, features],
+                            start=(k == 0),
+                            stop=(k == PASSES - 1),
+                        )
+
+        def add_bias(g, c):
+            if g not in biased:
+                biased[g] = rotate.tile([P, F, PACK], F32, name="biased")
+            features = slice(c * P, (c + 1) * P)
+            nc.vector.tensor_tensor(
+                out=biased[g][:, features, :],
+                in0=pre_banks[(g, c)][:].rearrange("p t f -> p f t"),
+                in1=bias_all[:, features].unsqueeze(2).to_broadcast([P, P, PACK]),
+                op=ALU.add,
+            )
+
+        def sum_squares(g, t):
+            if g not in square_sums:
+                square_sums[g] = keep.tile([P, PACK], F32, name="square_sums%d" % g)
+            squares = rotate.tile([P, D], BF16, name="squares")
+            nc.scalar.activation(
+                out=squares[:], in_=s_in[g][:, t, :], func=ACT.Square,
+                accum_out=square_sums[g][:, t : t + 1],
+            )
+
+        magnitudes = {}
+
+        def root_of_sums(g):
+            magnitudes[g] = keep.tile([P, PACK], F32, name="magnitudes%d" % g)
+            nc.gpsimd.tensor_tensor(
+                out=magnitudes[g][:], in0=square_sums[g][:], in1=half[:], op=ALU.pow
+            )
+
+        def make_gate(g):
+            s = keep.tile([P, PACK], F32, name="s%d" % g)
+            nc.scalar.activation(
+                out=s[:], in_=magnitudes[g][:], func=ACT.Sigmoid,
+                scale=gate_consts[:, GAIN_COL : GAIN_COL + 1],
+                bias=gate_consts[:, BIAS_COL : BIAS_COL + 1],
+            )
+            gates[g] = keep.tile([P, PACK], F32, name="gates%d" % g)
+            nc.gpsimd.tensor_tensor(out=gates[g][:], in0=s[:], in1=half[:], op=ALU.pow)
+
+        def apply_gate(g):
+            weighted[g] = rotate.tile([P, F, PACK], BF16, name="weighted", align_bytes=64)
+            nc.vector.tensor_tensor(
+                out=weighted[g][:], in0=biased[g][:],
+                in1=gates[g][:].unsqueeze(1).to_broadcast([P, F, PACK]), op=ALU.mult,
+            )
+
+        def quantise_weighted(g):
+            weighted_words[g] = keep.tile([P, F], U32, name="weighted_words%d" % g, align_bytes=64)
+            weighted_scales[g] = keep.tile([P, F], U8, name="weighted_scales%d" % g, align_bytes=64)
+            nc.vector.quantize_mx(
+                out=weighted_words[g][:].bitcast(FP8X4), scales=weighted_scales[g][:],
+                in_=weighted[g][:].rearrange("p f t -> p (f t)"),
+            )
+
+        def gram(g):
+            opens = g % 2 == 0
+            for m in range(CHUNKS):
+                if opens:
+                    gram_banks[m] = bank(gram_bank + m, [P, F], "gram")
+                rows = slice(m * P, (m + 1) * P)
+                nc.tensor.matmul_mx(
+                    out=gram_banks[m][:],
+                    lhsT=weighted_words[g][:, rows].bitcast(FP8X4),
+                    lhsT_scale=weighted_scales[g][:, rows],
+                    rhs=weighted_words[g][:].bitcast(FP8X4),
+                    rhs_scale=weighted_scales[g][:],
+                    start=opens,
+                    stop=not opens,
+                )
+
+        def store(sample, m, on_vector):
+            scaled = results.tile([P, F], F32, name="scaled")
+            if on_vector:
+                nc.vector.tensor_scalar_mul(
+                    out=scaled[:], in0=gram_banks[m][:], scalar1=1.0 / TOKENS
+                )
+            else:
+                nc.scalar.mul(out=scaled[:], in_=gram_banks[m][:], mul=1.0 / TOKENS)
+            nc.sync.dma_start(out=out[sample, m * P : (m + 1) * P, :], in_=scaled[:])
+
+        for c in range(CHUNKS):
+            transpose_pairs(("w", c), w_in[:, c, :], c)
+            copy_out(
+                ("w", c), w_grouped_pairs[:, :, c * P : (c + 1) * P, :], c in W_CHUNKS_ON_VECTOR
+            )
+        nc.vector.quantize_mx(
+            out=w_words[:].bitcast(FP8X4), scales=w_scales[:], in_=w_grouped[:]
+        )
+        spread = bank(0, [P, F], "spread")
+        nc.tensor.matmul(out=spread[:], lhsT=ones[:], rhs=const_row[:, 0:F], start=True, stop=True)
+        nc.vector.tensor_copy(out=bias_all[:], in_=spread[:])
+        spread_consts = bank(1, [P, CONST_COLS], "spread_consts")
+        nc.tensor.matmul(
+            out=spread_consts[:], lhsT=ones[:], rhs=const_row[:, F : F + CONST_COLS],
+            start=True, stop=True,
+        )
+        nc.vector.tensor_copy(out=gate_consts[:], in_=spread_consts[:])
+        for t in range(PACK):
+            transpose_pairs((0, t), h_in[0][:, t, :], gram_bank + t)
+            copy_out_slice(0, t)
+        for first in (0, 2):
+            quantise_h(0, first)
+            project(0, first)
+        for t in range(PACK):
+            sum_squares(0, t)
+        root_of_sums(0)
+
+        for r in range(GROUPS):
+            ahead = r + 1
+            for c in range(CHUNKS):
+                add_bias(r, c)
+                if ahead < GROUPS:
+                    transpose_pairs((ahead, c), h_in[ahead][:, c, :], gram_bank + c if r == 0 else c)
+            if ahead < GROUPS:
+                for t in range(ROWS_BEFORE_SIGMOID):
+                    sum_squares(ahead, t)
+                make_gate(r)
+                for t in range(PACK):
+                    copy_out_slice(ahead, t)
+                for t in range(ROWS_BEFORE_SIGMOID, PACK):
+                    sum_squares(ahead, t)
+                root_of_sums(ahead)
+            else:
+                for m in range(CHUNKS):
+                    if m == STORES_BEFORE_LAST_SIGMOID:
+                        make_gate(r)
+                    store(0, m, False)
+            if r >= 1:
+                quantise_weighted(r - 1)
+                gram(r - 1)
+            if ahead < GROUPS:
+                for first in (0, 2):
+                    quantise_h(ahead, first)
+                    project(ahead, first)
+            apply_gate(r)
+        quantise_weighted(GROUPS - 1)
+        gram(GROUPS - 1)
+        for m in range(CHUNKS):
+            store(1, m, m % 2 == 1)

@@ -21,7 +21,9 @@ CHUNKS = F // P
 FLOPS = 2 * SAMPLES * TOKENS * D * F + 2 * SAMPLES * F * F * TOKENS
 
 W_CHUNKS_ON_VECTOR = (0, 2)
-SLICES_ON_VECTOR = ((2, 3), (0, 2), (0,), (0,))
+SLICES_ON_VECTOR = ((),(0,2),(0,),(0,))
+SQUARES_ON_VECTOR = ((3,),(),(),())
+SCALAR_ORDER = [["c0","c1","c2","c3","g","s0","s1","s2","s3"],["s0","g","c0","c1","c2","c3","s1","s2","s3"],["s0","g","c0","c1","c2","c3","s1","s2","s3"]]
 ROWS_BEFORE_SIGMOID = 2
 STORES_BEFORE_LAST_SIGMOID = 3
 
@@ -136,10 +138,10 @@ def tile_proceduralmemory_pa_kernel(
             )
 
         def project(g, first):
-            for t in (first, first + 1):
-                for c in range(CHUNKS):
-                    if (g, c) not in pre_banks:
-                        pre_banks[(g, c)] = bank(c, [P, PACK, P], "pre")
+            for c in range(CHUNKS):
+                if (g, c) not in pre_banks:
+                    pre_banks[(g, c)] = bank(c, [P, PACK, P], "pre")
+                for t in (first, first + 1):
                     for k in range(PASSES):
                         tokens = slice(t * slice_words + k * P, t * slice_words + (k + 1) * P)
                         features = slice(k * F + c * P, k * F + (c + 1) * P)
@@ -167,11 +169,18 @@ def tile_proceduralmemory_pa_kernel(
         def sum_squares(g, t):
             if g not in square_sums:
                 square_sums[g] = keep.tile([P, PACK], F32, name="square_sums%d" % g)
-            squares = rotate.tile([P, D], BF16, name="squares")
-            nc.scalar.activation(
-                out=squares[:], in_=s_in[g][:, t, :], func=ACT.Square,
-                accum_out=square_sums[g][:, t : t + 1],
-            )
+            rows, total = s_in[g][:, t, :], square_sums[g][:, t : t + 1]
+            if t in SQUARES_ON_VECTOR[g]:
+                squares = rotate.tile([P, D], BF16, name="squares_v")
+                nc.vector.scalar_tensor_tensor(
+                    out=squares[:], in0=rows, scalar=1.0, in1=rows, op0=ALU.mult, op1=ALU.mult,
+                    accum_out=total,
+                )
+            else:
+                squares = rotate.tile([P, D], BF16, name="squares")
+                nc.scalar.activation(
+                    out=squares[:], in_=rows, func=ACT.Square, accum_out=total
+                )
 
         magnitudes = {}
 
@@ -240,22 +249,27 @@ def tile_proceduralmemory_pa_kernel(
         nc.vector.quantize_mx(
             out=w_words[:].bitcast(FP8X4), scales=w_scales[:], in_=w_grouped[:]
         )
+        for t in range(PACK):
+            transpose_pairs((0, t), h_in[0][:, t, :], gram_bank + t)
         spread = bank(0, [P, F], "spread")
         nc.tensor.matmul(out=spread[:], lhsT=ones[:], rhs=const_row[:, 0:F], start=True, stop=True)
-        nc.vector.tensor_copy(out=bias_all[:], in_=spread[:])
         spread_consts = bank(1, [P, CONST_COLS], "spread_consts")
         nc.tensor.matmul(
             out=spread_consts[:], lhsT=ones[:], rhs=const_row[:, F : F + CONST_COLS],
             start=True, stop=True,
         )
-        nc.vector.tensor_copy(out=gate_consts[:], in_=spread_consts[:])
         for t in range(PACK):
-            transpose_pairs((0, t), h_in[0][:, t, :], gram_bank + t)
             copy_out_slice(0, t)
+        quantise_h(0, 0)
+        nc.vector.tensor_copy(out=bias_all[:], in_=spread[:])
+        nc.vector.tensor_copy(out=gate_consts[:], in_=spread_consts[:])
+        quantise_h(0, 2)
         for first in (0, 2):
-            quantise_h(0, first)
             project(0, first)
         for t in range(PACK):
+            if t not in SQUARES_ON_VECTOR[0]:
+                sum_squares(0, t)
+        for t in SQUARES_ON_VECTOR[0]:
             sum_squares(0, t)
         root_of_sums(0)
 
@@ -266,13 +280,13 @@ def tile_proceduralmemory_pa_kernel(
                 if ahead < GROUPS:
                     transpose_pairs((ahead, c), h_in[ahead][:, c, :], gram_bank + c if r == 0 else c)
             if ahead < GROUPS:
-                for t in range(ROWS_BEFORE_SIGMOID):
-                    sum_squares(ahead, t)
-                make_gate(r)
-                for t in range(PACK):
-                    copy_out_slice(ahead, t)
-                for t in range(ROWS_BEFORE_SIGMOID, PACK):
-                    sum_squares(ahead, t)
+                for step in SCALAR_ORDER[r]:
+                    if step == "g":
+                        make_gate(r)
+                    elif step[0] == "c":
+                        copy_out_slice(ahead, int(step[1]))
+                    else:
+                        sum_squares(ahead, int(step[1]))
                 root_of_sums(ahead)
             else:
                 for m in range(CHUNKS):

@@ -25,7 +25,7 @@ SLICES_ON_VECTOR = ((),(0,2),(0,),(0,))
 SQUARES_ON_VECTOR = ((3,),(),(),())
 SCALAR_ORDER = [["c0","c1","c2","c3","g","s0","s1","s2","s3"],["s0","g","c0","c1","c2","c3","s1","s2","s3"],["s0","g","c0","c1","c2","c3","s1","s2","s3"]]
 ROWS_BEFORE_SIGMOID = 2
-STORES_BEFORE_LAST_SIGMOID = 3
+STORES_BEFORE_LAST_SIGMOID = 1
 
 GAIN_COL, BIAS_COL, CONST_COLS = 0, 16, 64
 
@@ -41,6 +41,7 @@ def tile_proceduralmemory_pa_kernel(
         rotate = ctx.enter_context(tc.tile_pool(name="rotate", bufs=2))
         keep = ctx.enter_context(tc.tile_pool(name="keep", bufs=1))
         results = ctx.enter_context(tc.tile_pool(name="results", bufs=CHUNKS))
+        halves = ctx.enter_context(tc.tile_pool(name="halves", bufs=2 * CHUNKS))
         psum = ctx.enter_context(tc.psum_pool(name="psum", bufs=1))
 
         def bank(index, shape, name):
@@ -72,7 +73,9 @@ def tile_proceduralmemory_pa_kernel(
         s_view = surprise.rearrange("b (g p t) d -> (b g) p t d", p=P, t=PACK)
         h_in = [inputs.tile([P, PACK, D], BF16, name="h_in%d" % g) for g in range(GROUPS)]
         s_in = [inputs.tile([P, PACK, D], BF16, name="s_in%d" % g) for g in range(GROUPS)]
-        for c in range(CHUNKS):
+        for part in (slice(0, D // 2), slice(D // 2, D)):
+            nc.sync.dma_start(out=w_in[:, 0, part], in_=w_view[:, 0, part])
+        for c in range(1, CHUNKS):
             nc.sync.dma_start(out=w_in[:, c, :], in_=w_view[:, c, :])
         for t in range(PACK):
             nc.sync.dma_start(out=h_in[0][:, t, :], in_=h_view[0][:, t, :])
@@ -200,19 +203,44 @@ def tile_proceduralmemory_pa_kernel(
             gates[g] = keep.tile([P, PACK], F32, name="gates%d" % g)
             nc.gpsimd.tensor_tensor(out=gates[g][:], in0=s[:], in1=half[:], op=ALU.pow)
 
-        def apply_gate(g):
-            weighted[g] = rotate.tile([P, F, PACK], BF16, name="weighted", align_bytes=64)
+        def apply_gate(g, first=0, last=CHUNKS):
+            if g not in weighted:
+                weighted[g] = rotate.tile([P, F, PACK], BF16, name="weighted", align_bytes=64)
+            features = slice(first * P, last * P)
             nc.vector.tensor_tensor(
-                out=weighted[g][:], in0=biased[g][:],
-                in1=gates[g][:].unsqueeze(1).to_broadcast([P, F, PACK]), op=ALU.mult,
+                out=weighted[g][:, features, :], in0=biased[g][:, features, :],
+                in1=gates[g][:].unsqueeze(1).to_broadcast([P, (last - first) * P, PACK]), op=ALU.mult,
             )
 
-        def quantise_weighted(g):
-            weighted_words[g] = keep.tile([P, F], U32, name="weighted_words%d" % g, align_bytes=64)
-            weighted_scales[g] = keep.tile([P, F], U8, name="weighted_scales%d" % g, align_bytes=64)
+        def apply_gate_on_scalar(g, c):
+            features = slice(c * P, (c + 1) * P)
+            for t in range(PACK):
+                nc.scalar.activation(
+                    out=weighted[g][:, features, t], in_=biased[g][:, features, t], func=ACT.Copy,
+                    scale=gates[g][:, t : t + 1],
+                )
+
+        def quantise_weighted(g, first=0, last=CHUNKS):
+            if g not in weighted_words:
+                weighted_words[g] = keep.tile([P, F], U32, name="weighted_words%d" % g, align_bytes=64)
+                weighted_scales[g] = keep.tile([P, F], U8, name="weighted_scales%d" % g, align_bytes=64)
+            features = slice(first * P, last * P)
             nc.vector.quantize_mx(
-                out=weighted_words[g][:].bitcast(FP8X4), scales=weighted_scales[g][:],
-                in_=weighted[g][:].rearrange("p f t -> p (f t)"),
+                out=weighted_words[g][:, features].bitcast(FP8X4), scales=weighted_scales[g][:, features],
+                in_=weighted[g][:].rearrange("p f t -> p (f t)")[:, first * P * PACK : last * P * PACK],
+            )
+
+        def close_gram(m, half):
+            g = GROUPS - 1
+            rows, cols = slice(m * P, (m + 1) * P), slice(half * 2 * P, (half + 1) * 2 * P)
+            nc.tensor.matmul_mx(
+                out=gram_banks[m][:, cols],
+                lhsT=weighted_words[g][:, rows].bitcast(FP8X4),
+                lhsT_scale=weighted_scales[g][:, rows],
+                rhs=weighted_words[g][:, cols].bitcast(FP8X4),
+                rhs_scale=weighted_scales[g][:, cols],
+                start=False,
+                stop=True,
             )
 
         def gram(g):
@@ -231,6 +259,22 @@ def tile_proceduralmemory_pa_kernel(
                     stop=not opens,
                 )
 
+        def gram_half(g, m, half):
+            opens = g % 2 == 0
+            if opens:
+                gram_banks[(m, half)] = bank(gram_bank + m if half == 0 else m, [P, F // 2], "gram_half")
+            rows = slice(m * P, (m + 1) * P)
+            cols = slice(half * (F // 2), (half + 1) * (F // 2))
+            nc.tensor.matmul_mx(
+                out=gram_banks[(m, half)][:],
+                lhsT=weighted_words[g][:, rows].bitcast(FP8X4),
+                lhsT_scale=weighted_scales[g][:, rows],
+                rhs=weighted_words[g][:, cols].bitcast(FP8X4),
+                rhs_scale=weighted_scales[g][:, cols],
+                start=opens,
+                stop=not opens,
+            )
+
         def store(sample, m, on_vector):
             scaled = results.tile([P, F], F32, name="scaled")
             if on_vector:
@@ -240,6 +284,17 @@ def tile_proceduralmemory_pa_kernel(
             else:
                 nc.scalar.mul(out=scaled[:], in_=gram_banks[m][:], mul=1.0 / TOKENS)
             nc.sync.dma_start(out=out[sample, m * P : (m + 1) * P, :], in_=scaled[:])
+
+        def store_half(sample, m, half, on_vector):
+            cols = slice(half * (F // 2), (half + 1) * (F // 2))
+            scaled = halves.tile([P, F // 2], F32, name="scaled_half")
+            if on_vector:
+                nc.vector.tensor_scalar_mul(
+                    out=scaled[:], in0=gram_banks[(m, half)][:], scalar1=1.0 / TOKENS
+                )
+            else:
+                nc.scalar.mul(out=scaled[:], in_=gram_banks[(m, half)][:], mul=1.0 / TOKENS)
+            nc.sync.dma_start(out=out[sample, m * P : (m + 1) * P, cols], in_=scaled[:])
 
         for c in range(CHUNKS):
             transpose_pairs(("w", c), w_in[:, c, :], c)
@@ -295,13 +350,27 @@ def tile_proceduralmemory_pa_kernel(
                     store(0, m, False)
             if r >= 1:
                 quantise_weighted(r - 1)
-                gram(r - 1)
+                if r < GROUPS - 1:
+                    gram(r - 1)
+                else:
+                    for half in (0, 1):
+                        for m in range(CHUNKS):
+                            gram_half(r - 1, m, half)
             if ahead < GROUPS:
                 for first in (0, 2):
                     quantise_h(ahead, first)
                     project(ahead, first)
-            apply_gate(r)
-        quantise_weighted(GROUPS - 1)
-        gram(GROUPS - 1)
-        for m in range(CHUNKS):
-            store(1, m, m % 2 == 1)
+            if ahead < GROUPS:
+                apply_gate(r)
+        g = GROUPS - 1
+        apply_gate(g, 0, 2)
+        apply_gate(g, 2, 3)
+        quantise_weighted(g, 0, 2)
+        apply_gate_on_scalar(g, 3)
+        quantise_weighted(g, 2, 4)
+        for half in (0, 1):
+            for m in range(CHUNKS):
+                gram_half(g, m, half)
+        for half in (0, 1):
+            for m in range(CHUNKS):
+                store_half(1, m, half, m % 2 == 1)

@@ -18,14 +18,9 @@ GROUP = P * PACK
 GROUPS = SAMPLES * TOKENS // GROUP
 PASSES = D // (P * PACK)
 CHUNKS = F // P
+HALF = F // 2
+WORDS = PASSES * P
 FLOPS = 2 * SAMPLES * TOKENS * D * F + 2 * SAMPLES * F * F * TOKENS
-
-W_CHUNKS_ON_VECTOR = (0, 2)
-SLICES_ON_VECTOR = ((),(0,2),(0,),(0,))
-SQUARES_ON_VECTOR = ((3,),(),(),())
-SCALAR_ORDER = [["c0","c1","c2","c3","g","s0","s1","s2","s3"],["s0","g","c0","c1","c2","c3","s1","s2","s3"],["s0","g","c0","c1","c2","c3","s1","s2","s3"]]
-ROWS_BEFORE_SIGMOID = 2
-STORES_BEFORE_LAST_SIGMOID = 1
 
 GAIN_COL, BIAS_COL, CONST_COLS = 0, 16, 64
 
@@ -44,10 +39,10 @@ def tile_proceduralmemory_pa_kernel(
         halves = ctx.enter_context(tc.tile_pool(name="halves", bufs=2 * CHUNKS))
         psum = ctx.enter_context(tc.psum_pool(name="psum", bufs=1))
 
-        def bank(index, shape, name):
-            return psum.tile(shape, F32, name=name, tag="bank%d" % index)
+        def bank(index, shape, name, dtype=F32):
+            return psum.tile(shape, dtype, name=name, tag="bank%d" % index)
 
-        gram_bank = CHUNKS
+        upper = CHUNKS
 
         const_row = const.tile([P, F + CONST_COLS], BF16, name="const_row")
         nc.vector.memset(const_row[:], 0.0)
@@ -73,32 +68,33 @@ def tile_proceduralmemory_pa_kernel(
         s_view = surprise.rearrange("b (g p t) d -> (b g) p t d", p=P, t=PACK)
         h_in = [inputs.tile([P, PACK, D], BF16, name="h_in%d" % g) for g in range(GROUPS)]
         s_in = [inputs.tile([P, PACK, D], BF16, name="s_in%d" % g) for g in range(GROUPS)]
+
+        def load_slices(dst, src, g, count):
+            for t in range(0, PACK, count):
+                nc.sync.dma_start(
+                    out=dst[g][:, t : t + count, :], in_=src[g][:, t : t + count, :]
+                )
+
         for part in (slice(0, D // 2), slice(D // 2, D)):
             nc.sync.dma_start(out=w_in[:, 0, part], in_=w_view[:, 0, part])
         for c in range(1, CHUNKS):
             nc.sync.dma_start(out=w_in[:, c, :], in_=w_view[:, c, :])
-        for t in range(PACK):
-            nc.sync.dma_start(out=h_in[0][:, t, :], in_=h_view[0][:, t, :])
-        for t in range(PACK):
-            nc.sync.dma_start(out=s_in[0][:, t, :], in_=s_view[0][:, t, :])
-        for g in range(1, GROUPS):
-            nc.sync.dma_start(out=h_in[g][:], in_=h_view[g])
-            nc.sync.dma_start(out=s_in[g][:], in_=s_view[g])
+        for g in range(GROUPS):
+            count = 1 if g < 2 else 2
+            load_slices(h_in, h_view, g, count)
+            load_slices(s_in, s_view, g, count)
 
-        bias_all = const.tile([P, F], F32, name="bias_all")
+        bias_all = const.tile([P, F], BF16, name="bias_all")
         gate_consts = const.tile([P, CONST_COLS], F32, name="gate_consts")
-        w_grouped = keep.tile([P, PASSES * F * PACK], BF16, name="w_grouped", align_bytes=64)
-        w_grouped_pairs = w_grouped[:].bitcast(F32).rearrange(
-            "p (k f u) -> p k f u", k=PASSES, f=F, u=2
-        )
-        w_words = keep.tile([P, PASSES * F], U32, name="w_words", align_bytes=64)
-        w_scales = keep.tile([P, PASSES * F], U8, name="w_scales", align_bytes=64)
+        w_grouped = keep.tile([P, CHUNKS * WORDS * PACK], BF16, name="w_grouped", align_bytes=64)
+        w_words = keep.tile([P, CHUNKS * WORDS], U32, name="w_words", align_bytes=64)
+        w_scales = keep.tile([P, CHUNKS * WORDS], U8, name="w_scales", align_bytes=64)
 
         flipped = {}
         h_grouped, h_words, h_scales = {}, {}, {}
         pre_banks = {}
         biased, weighted, weighted_words, weighted_scales = {}, {}, {}, {}
-        square_sums, gates = {}, {}
+        square_sums, magnitudes, gates = {}, {}, {}
         gram_banks = {}
 
         def transpose_pairs(key, rows, index):
@@ -108,36 +104,39 @@ def tile_proceduralmemory_pa_kernel(
                 nc.tensor.transpose(planes[:, j, :], pairs[:, j * P : (j + 1) * P], identity[:])
             flipped[key] = planes
 
-        def copy_out(key, grouped_pairs, on_vector):
+        def copy_out(key, grouped, on_vector):
+            pairs = grouped.bitcast(F32).rearrange("p (k r u) -> p k r u", k=PASSES, r=P, u=2)
             alternating = flipped[key][:].rearrange("p (k u) r -> p k r u", u=2)
             if on_vector:
-                nc.vector.tensor_copy(out=grouped_pairs, in_=alternating)
+                nc.vector.tensor_copy(out=pairs, in_=alternating)
             else:
-                nc.scalar.copy(out=grouped_pairs, in_=alternating)
+                nc.scalar.copy(out=pairs, in_=alternating)
 
-        def copy_out_slice(g, t):
+        def copy_w(c, on_vector):
+            copy_out(("w", c), w_grouped[:, c * WORDS * PACK : (c + 1) * WORDS * PACK], on_vector)
+
+        def quantise_w(first):
+            words = slice(first * WORDS, (first + 2) * WORDS)
+            nc.vector.quantize_mx(
+                out=w_words[:, words].bitcast(FP8X4), scales=w_scales[:, words],
+                in_=w_grouped[:, first * WORDS * PACK : (first + 2) * WORDS * PACK],
+            )
+
+        def copy_h(g, t, on_vector):
             if g not in h_grouped:
                 h_grouped[g] = rotate.tile(
-                    [P, PACK * PASSES * P * PACK], BF16, name="h_grouped", align_bytes=64
+                    [P, PACK * WORDS * PACK], BF16, name="h_grouped", align_bytes=64
                 )
-            pairs = h_grouped[g][:].bitcast(F32).rearrange(
-                "p (t k r u) -> p t k r u", t=PACK, k=PASSES, r=P, u=2
-            )
-            copy_out((g, t), pairs[:, t], t in SLICES_ON_VECTOR[g])
-
-        slice_words = PASSES * P
+            copy_out((g, t), h_grouped[g][:, t * WORDS * PACK : (t + 1) * WORDS * PACK], on_vector)
 
         def quantise_h(g, first):
             if g not in h_words:
-                h_words[g] = rotate.tile([P, PACK * slice_words], U32, name="h_words", align_bytes=64)
-                h_scales[g] = rotate.tile(
-                    [P, PACK * slice_words], U8, name="h_scales", align_bytes=64
-                )
-            cols = slice(first * slice_words, (first + 2) * slice_words)
+                h_words[g] = rotate.tile([P, PACK * WORDS], U32, name="h_words", align_bytes=64)
+                h_scales[g] = rotate.tile([P, PACK * WORDS], U8, name="h_scales", align_bytes=64)
+            words = slice(first * WORDS, (first + 2) * WORDS)
             nc.vector.quantize_mx(
-                out=h_words[g][:, cols].bitcast(FP8X4),
-                scales=h_scales[g][:, cols],
-                in_=h_grouped[g][:, first * slice_words * PACK : (first + 2) * slice_words * PACK],
+                out=h_words[g][:, words].bitcast(FP8X4), scales=h_scales[g][:, words],
+                in_=h_grouped[g][:, first * WORDS * PACK : (first + 2) * WORDS * PACK],
             )
 
         def project(g, first):
@@ -146,8 +145,8 @@ def tile_proceduralmemory_pa_kernel(
                     pre_banks[(g, c)] = bank(c, [P, PACK, P], "pre")
                 for t in (first, first + 1):
                     for k in range(PASSES):
-                        tokens = slice(t * slice_words + k * P, t * slice_words + (k + 1) * P)
-                        features = slice(k * F + c * P, k * F + (c + 1) * P)
+                        tokens = slice(t * WORDS + k * P, t * WORDS + (k + 1) * P)
+                        features = slice(c * WORDS + k * P, c * WORDS + (k + 1) * P)
                         nc.tensor.matmul_mx(
                             out=pre_banks[(g, c)][:, t, :],
                             lhsT=h_words[g][:, tokens].bitcast(FP8X4),
@@ -169,23 +168,19 @@ def tile_proceduralmemory_pa_kernel(
                 op=ALU.add,
             )
 
-        def sum_squares(g, t):
+        def sum_squares(g, t, on_vector=False):
             if g not in square_sums:
                 square_sums[g] = keep.tile([P, PACK], F32, name="square_sums%d" % g)
             rows, total = s_in[g][:, t, :], square_sums[g][:, t : t + 1]
-            if t in SQUARES_ON_VECTOR[g]:
-                squares = rotate.tile([P, D], BF16, name="squares_v")
+            if on_vector:
+                unused = rotate.tile([P, D], BF16, name="unused_v")
                 nc.vector.scalar_tensor_tensor(
-                    out=squares[:], in0=rows, scalar=1.0, in1=rows, op0=ALU.mult, op1=ALU.mult,
+                    out=unused[:], in0=rows, scalar=1.0, in1=rows, op0=ALU.mult, op1=ALU.mult,
                     accum_out=total,
                 )
             else:
-                squares = rotate.tile([P, D], BF16, name="squares")
-                nc.scalar.activation(
-                    out=squares[:], in_=rows, func=ACT.Square, accum_out=total
-                )
-
-        magnitudes = {}
+                unused = rotate.tile([P, D], BF16, name="unused_s")
+                nc.scalar.activation(out=unused[:], in_=rows, func=ACT.Square, accum_out=total)
 
         def root_of_sums(g):
             magnitudes[g] = keep.tile([P, PACK], F32, name="magnitudes%d" % g)
@@ -203,13 +198,14 @@ def tile_proceduralmemory_pa_kernel(
             gates[g] = keep.tile([P, PACK], F32, name="gates%d" % g)
             nc.gpsimd.tensor_tensor(out=gates[g][:], in0=s[:], in1=half[:], op=ALU.pow)
 
-        def apply_gate(g, first=0, last=CHUNKS):
+        def apply_gate(g, first, last):
             if g not in weighted:
                 weighted[g] = rotate.tile([P, F, PACK], BF16, name="weighted", align_bytes=64)
             features = slice(first * P, last * P)
             nc.vector.tensor_tensor(
                 out=weighted[g][:, features, :], in0=biased[g][:, features, :],
-                in1=gates[g][:].unsqueeze(1).to_broadcast([P, (last - first) * P, PACK]), op=ALU.mult,
+                in1=gates[g][:].unsqueeze(1).to_broadcast([P, (last - first) * P, PACK]),
+                op=ALU.mult,
             )
 
         def apply_gate_on_scalar(g, c):
@@ -220,111 +216,78 @@ def tile_proceduralmemory_pa_kernel(
                     scale=gates[g][:, t : t + 1],
                 )
 
-        def quantise_weighted(g, first=0, last=CHUNKS):
+        def quantise_weighted(g, first, last):
             if g not in weighted_words:
                 weighted_words[g] = keep.tile([P, F], U32, name="weighted_words%d" % g, align_bytes=64)
                 weighted_scales[g] = keep.tile([P, F], U8, name="weighted_scales%d" % g, align_bytes=64)
             features = slice(first * P, last * P)
             nc.vector.quantize_mx(
-                out=weighted_words[g][:, features].bitcast(FP8X4), scales=weighted_scales[g][:, features],
-                in_=weighted[g][:].rearrange("p f t -> p (f t)")[:, first * P * PACK : last * P * PACK],
+                out=weighted_words[g][:, features].bitcast(FP8X4),
+                scales=weighted_scales[g][:, features],
+                in_=weighted[g][:, features, :].rearrange("p f t -> p (f t)"),
             )
 
-        def close_gram(m, half):
-            g = GROUPS - 1
-            rows, cols = slice(m * P, (m + 1) * P), slice(half * 2 * P, (half + 1) * 2 * P)
-            nc.tensor.matmul_mx(
-                out=gram_banks[m][:, cols],
-                lhsT=weighted_words[g][:, rows].bitcast(FP8X4),
-                lhsT_scale=weighted_scales[g][:, rows],
-                rhs=weighted_words[g][:, cols].bitcast(FP8X4),
-                rhs_scale=weighted_scales[g][:, cols],
-                start=False,
-                stop=True,
-            )
-
-        def gram(g):
-            opens = g % 2 == 0
-            for m in range(CHUNKS):
-                if opens:
-                    gram_banks[m] = bank(gram_bank + m, [P, F], "gram")
-                rows = slice(m * P, (m + 1) * P)
-                nc.tensor.matmul_mx(
-                    out=gram_banks[m][:],
-                    lhsT=weighted_words[g][:, rows].bitcast(FP8X4),
-                    lhsT_scale=weighted_scales[g][:, rows],
-                    rhs=weighted_words[g][:].bitcast(FP8X4),
-                    rhs_scale=weighted_scales[g][:],
-                    start=opens,
-                    stop=not opens,
-                )
-
-        def gram_half(g, m, half):
-            opens = g % 2 == 0
-            if opens:
-                gram_banks[(m, half)] = bank(gram_bank + m if half == 0 else m, [P, F // 2], "gram_half")
+        def gram_pass(g, m, sums, cols):
             rows = slice(m * P, (m + 1) * P)
-            cols = slice(half * (F // 2), (half + 1) * (F // 2))
             nc.tensor.matmul_mx(
-                out=gram_banks[(m, half)][:],
+                out=sums,
                 lhsT=weighted_words[g][:, rows].bitcast(FP8X4),
                 lhsT_scale=weighted_scales[g][:, rows],
                 rhs=weighted_words[g][:, cols].bitcast(FP8X4),
                 rhs_scale=weighted_scales[g][:, cols],
-                start=opens,
-                stop=not opens,
+                start=(g % 2 == 0),
+                stop=(g % 2 == 1),
             )
 
-        def store(sample, m, on_vector):
-            scaled = results.tile([P, F], F32, name="scaled")
-            if on_vector:
-                nc.vector.tensor_scalar_mul(
-                    out=scaled[:], in0=gram_banks[m][:], scalar1=1.0 / TOKENS
-                )
-            else:
-                nc.scalar.mul(out=scaled[:], in_=gram_banks[m][:], mul=1.0 / TOKENS)
-            nc.sync.dma_start(out=out[sample, m * P : (m + 1) * P, :], in_=scaled[:])
+        def gram_first_sample(g):
+            for m in range(CHUNKS):
+                if g == 0:
+                    gram_banks[m] = bank(upper + m, [P, F], "gram")
+                gram_pass(g, m, gram_banks[m][:], slice(0, F))
 
-        def store_half(sample, m, half, on_vector):
-            cols = slice(half * (F // 2), (half + 1) * (F // 2))
-            scaled = halves.tile([P, F // 2], F32, name="scaled_half")
+        def gram_second_sample(g):
+            for h in range(2):
+                for m in range(CHUNKS):
+                    if g == 2:
+                        gram_banks[(m, h)] = bank(upper + m if h == 0 else m, [P, HALF], "gram_half")
+                    gram_pass(g, m, gram_banks[(m, h)][:], slice(h * HALF, (h + 1) * HALF))
+
+        def store(sample, m, cols, sums, pool, name, on_vector):
+            scaled = pool.tile([P, cols.stop - cols.start], F32, name=name)
             if on_vector:
-                nc.vector.tensor_scalar_mul(
-                    out=scaled[:], in0=gram_banks[(m, half)][:], scalar1=1.0 / TOKENS
-                )
+                nc.vector.tensor_scalar_mul(out=scaled[:], in0=sums[:], scalar1=1.0 / TOKENS)
             else:
-                nc.scalar.mul(out=scaled[:], in_=gram_banks[(m, half)][:], mul=1.0 / TOKENS)
+                nc.scalar.mul(out=scaled[:], in_=sums[:], mul=1.0 / TOKENS)
             nc.sync.dma_start(out=out[sample, m * P : (m + 1) * P, cols], in_=scaled[:])
 
         for c in range(CHUNKS):
             transpose_pairs(("w", c), w_in[:, c, :], c)
-            copy_out(
-                ("w", c), w_grouped_pairs[:, :, c * P : (c + 1) * P, :], c in W_CHUNKS_ON_VECTOR
-            )
-        nc.vector.quantize_mx(
-            out=w_words[:].bitcast(FP8X4), scales=w_scales[:], in_=w_grouped[:]
-        )
         for t in range(PACK):
-            transpose_pairs((0, t), h_in[0][:, t, :], gram_bank + t)
-        spread = bank(0, [P, F], "spread")
+            transpose_pairs((0, t), h_in[0][:, t, :], upper + t)
+        copy_w(0, True)
+        copy_w(1, False)
+        copy_w(2, True)
+        copy_w(3, False)
+        quantise_w(0)
+        copy_h(0, 0, True)
+        quantise_w(2)
+        for t in range(1, PACK):
+            copy_h(0, t, False)
+        spread = bank(upper, [P, F], "spread", BF16)
         nc.tensor.matmul(out=spread[:], lhsT=ones[:], rhs=const_row[:, 0:F], start=True, stop=True)
-        spread_consts = bank(1, [P, CONST_COLS], "spread_consts")
+        spread_consts = bank(upper + 1, [P, CONST_COLS], "spread_consts")
         nc.tensor.matmul(
             out=spread_consts[:], lhsT=ones[:], rhs=const_row[:, F : F + CONST_COLS],
             start=True, stop=True,
         )
-        for t in range(PACK):
-            copy_out_slice(0, t)
         quantise_h(0, 0)
         nc.vector.tensor_copy(out=bias_all[:], in_=spread[:])
-        nc.vector.tensor_copy(out=gate_consts[:], in_=spread_consts[:])
         quantise_h(0, 2)
-        for first in (0, 2):
-            project(0, first)
-        for t in range(PACK):
-            if t not in SQUARES_ON_VECTOR[0]:
-                sum_squares(0, t)
-        for t in SQUARES_ON_VECTOR[0]:
+        nc.vector.tensor_copy(out=gate_consts[:], in_=spread_consts[:])
+        project(0, 0)
+        project(0, 2)
+        sum_squares(0, 0, on_vector=True)
+        for t in range(1, PACK):
             sum_squares(0, t)
         root_of_sums(0)
 
@@ -333,44 +296,47 @@ def tile_proceduralmemory_pa_kernel(
             for c in range(CHUNKS):
                 add_bias(r, c)
                 if ahead < GROUPS:
-                    transpose_pairs((ahead, c), h_in[ahead][:, c, :], gram_bank + c if r == 0 else c)
+                    transpose_pairs((ahead, c), h_in[ahead][:, c, :], upper + c if r == 0 else c)
             if ahead < GROUPS:
-                for step in SCALAR_ORDER[r]:
-                    if step == "g":
-                        make_gate(r)
-                    elif step[0] == "c":
-                        copy_out_slice(ahead, int(step[1]))
-                    else:
-                        sum_squares(ahead, int(step[1]))
+                if r == 0:
+                    for t in range(1, PACK):
+                        copy_h(ahead, t, False)
+                    make_gate(r)
+                    sum_squares(ahead, 0)
+                else:
+                    sum_squares(ahead, 0)
+                    copy_h(ahead, 1, False)
+                    make_gate(r)
+                    copy_h(ahead, 2, False)
+                    copy_h(ahead, 3, False)
+                for t in range(1, PACK):
+                    sum_squares(ahead, t)
                 root_of_sums(ahead)
+                copy_h(ahead, 0, True)
             else:
                 for m in range(CHUNKS):
-                    if m == STORES_BEFORE_LAST_SIGMOID:
+                    if m == 2:
                         make_gate(r)
-                    store(0, m, False)
+                    store(0, m, slice(0, F), gram_banks[m], results, "scaled", False)
             if r >= 1:
-                quantise_weighted(r - 1)
+                quantise_weighted(r - 1, 0, CHUNKS)
                 if r < GROUPS - 1:
-                    gram(r - 1)
+                    gram_first_sample(r - 1)
                 else:
-                    for half in (0, 1):
-                        for m in range(CHUNKS):
-                            gram_half(r - 1, m, half)
+                    gram_second_sample(r - 1)
             if ahead < GROUPS:
                 for first in (0, 2):
                     quantise_h(ahead, first)
                     project(ahead, first)
-            if ahead < GROUPS:
-                apply_gate(r)
-        g = GROUPS - 1
-        apply_gate(g, 0, 2)
-        apply_gate(g, 2, 3)
-        quantise_weighted(g, 0, 2)
-        apply_gate_on_scalar(g, 3)
-        quantise_weighted(g, 2, 4)
-        for half in (0, 1):
+                apply_gate(r, 0, CHUNKS)
+        last = GROUPS - 1
+        apply_gate(last, 0, 2)
+        apply_gate(last, 2, 3)
+        apply_gate_on_scalar(last, 3)
+        quantise_weighted(last, 0, 2)
+        quantise_weighted(last, 2, 4)
+        gram_second_sample(last)
+        for h in range(2):
             for m in range(CHUNKS):
-                gram_half(g, m, half)
-        for half in (0, 1):
-            for m in range(CHUNKS):
-                store_half(1, m, half, m % 2 == 1)
+                cols = slice(h * HALF, (h + 1) * HALF)
+                store(1, m, cols, gram_banks[(m, h)], halves, "scaled_half", m % 2 == 1)

@@ -298,21 +298,23 @@ def tile_proceduralmemory_pa_kernel(
                 if ahead < GROUPS:
                     transpose_pairs((ahead, c), h_in[ahead][:, c, :], upper + c if r == 0 else c)
             if ahead < GROUPS:
+                on_vector = (0, 3) if r == 0 else (0,)
+                on_scalar = [t for t in range(PACK) if t not in on_vector]
                 if r == 0:
-                    for t in range(1, PACK):
+                    for t in on_scalar:
                         copy_h(ahead, t, False)
                     make_gate(r)
                     sum_squares(ahead, 0)
                 else:
                     sum_squares(ahead, 0)
-                    copy_h(ahead, 1, False)
                     make_gate(r)
-                    copy_h(ahead, 2, False)
-                    copy_h(ahead, 3, False)
+                    for t in on_scalar:
+                        copy_h(ahead, t, False)
                 for t in range(1, PACK):
                     sum_squares(ahead, t)
                 root_of_sums(ahead)
-                copy_h(ahead, 0, True)
+                for t in on_vector:
+                    copy_h(ahead, t, True)
             else:
                 for m in range(CHUNKS):
                     if m == 2:

@@ -22,7 +22,7 @@ HALF = F // 2
 WORDS = PASSES * P
 FLOPS = 2 * SAMPLES * TOKENS * D * F + 2 * SAMPLES * F * F * TOKENS
 
-GAIN_COL, BIAS_COL, CONST_COLS = 0, 16, 64
+GAIN_COL, BIAS_COL, CONST_COLS = 0, 16, 32
 
 
 def tile_proceduralmemory_pa_kernel(
@@ -293,10 +293,13 @@ def tile_proceduralmemory_pa_kernel(
 
         for r in range(GROUPS):
             ahead = r + 1
+            if r < 2:
+                for t in range(PACK):
+                    transpose_pairs((ahead, t), h_in[ahead][:, t, :], upper + t)
             for c in range(CHUNKS):
                 add_bias(r, c)
-                if ahead < GROUPS:
-                    transpose_pairs((ahead, c), h_in[ahead][:, c, :], upper + c if r == 0 else c)
+                if r == 2:
+                    transpose_pairs((ahead, c), h_in[ahead][:, c, :], c)
             if ahead < GROUPS:
                 on_vector = (0, 3) if r == 0 else (0,)
                 on_scalar = [t for t in range(PACK) if t not in on_vector]

@@ -188,6 +188,13 @@ def tile_proceduralmemory_pa_kernel(
                 out=magnitudes[g][:], in0=square_sums[g][:], in1=half[:], op=ALU.pow
             )
 
+        def root_part(g, a, b):
+            if g not in magnitudes:
+                magnitudes[g] = keep.tile([P, PACK], F32, name="magnitudes%d" % g)
+            nc.gpsimd.tensor_tensor(
+                out=magnitudes[g][:, a:b], in0=square_sums[g][:, a:b], in1=half[:, a:b], op=ALU.pow
+            )
+
         def make_gate(g):
             s = keep.tile([P, PACK], F32, name="s%d" % g)
             nc.scalar.activation(
@@ -315,7 +322,12 @@ def tile_proceduralmemory_pa_kernel(
                         copy_h(ahead, t, False)
                 for t in range(1, PACK):
                     sum_squares(ahead, t)
-                root_of_sums(ahead)
+                    if ahead == 3 and t == 2:
+                        root_part(ahead, 0, 3)
+                if ahead == 3:
+                    root_part(ahead, 3, 4)
+                else:
+                    root_of_sums(ahead)
                 for t in on_vector:
                     copy_h(ahead, t, True)
             else:

from contextlib import ExitStack

import concourse.mybir as mybir
from concourse.masks import make_identity

F32 = mybir.dt.float32
BF16 = mybir.dt.bfloat16
U32 = mybir.dt.uint32
U8 = mybir.dt.uint8
FP8X4 = mybir.dt.float8_e4m3fn_x4
ALU = mybir.AluOpType
ACT = mybir.ActivationFunctionType

P = 128
SAMPLES, TOKENS, D, F = 2, 1024, 1024, 512
PACK = 4
GROUP = P * PACK
GROUPS = SAMPLES * TOKENS // GROUP
PASSES = D // (P * PACK)
CHUNKS = F // P
HALF = F // 2
WORDS = PASSES * P
FLOPS = 2 * SAMPLES * TOKENS * D * F + 2 * SAMPLES * F * F * TOKENS

GAIN_COL, BIAS_COL, CONST_COLS = 0, 16, 32


def tile_proceduralmemory_pa_kernel(
    tc, H, surprise, proj_in_w, proj_in_b, surp_scale, surp_bias, out
):
    nc = tc.nc
    with ExitStack() as ctx:
        ctx.enter_context(tc.manual_schedule())
        const = ctx.enter_context(tc.tile_pool(name="const", bufs=1))
        inputs = ctx.enter_context(tc.tile_pool(name="inputs", bufs=1))
        rotate = ctx.enter_context(tc.tile_pool(name="rotate", bufs=2))
        keep = ctx.enter_context(tc.tile_pool(name="keep", bufs=1))
        results = ctx.enter_context(tc.tile_pool(name="results", bufs=CHUNKS))
        halves = ctx.enter_context(tc.tile_pool(name="halves", bufs=2 * CHUNKS))
        psum = ctx.enter_context(tc.psum_pool(name="psum", bufs=1))

        def bank(index, shape, name, dtype=F32):
            return psum.tile(shape, dtype, name=name, tag="bank%d" % index)

        upper = CHUNKS

        const_row = const.tile([P, F + CONST_COLS], BF16, name="const_row")
        nc.vector.memset(const_row[:], 0.0)
        nc.scalar.dma_start(out=const_row[0:1, 0:F], in_=proj_in_b.unsqueeze(0))
        nc.scalar.dma_start(
            out=const_row[0:1, F + GAIN_COL : F + GAIN_COL + 1], in_=surp_scale.unsqueeze(0)
        )
        nc.scalar.dma_start(
            out=const_row[0:1, F + BIAS_COL : F + BIAS_COL + 1], in_=surp_bias.unsqueeze(0)
        )
        half = const.tile([P, PACK], F32, name="half")
        nc.vector.memset(half[:], 0.5)
        table_warm = const.tile([P, 1], F32, name="table_warm")
        nc.scalar.activation(out=table_warm[:], in_=half[:, 0:1], func=ACT.Sigmoid)
        ones = const.tile([P, P], BF16, name="ones")
        nc.vector.memset(ones[:], 1.0)
        identity = const.tile([P, P], F32, name="identity")
        make_identity(nc, identity[:])

        w_in = inputs.tile([P, CHUNKS, D], BF16, name="w_in")
        w_view = proj_in_w.rearrange("(c p) d -> p c d", p=P)
        h_view = H.rearrange("b (g p t) d -> (b g) p t d", p=P, t=PACK)
        s_view = surprise.rearrange("b (g p t) d -> (b g) p t d", p=P, t=PACK)
        h_in = [inputs.tile([P, PACK, D], BF16, name="h_in%d" % g) for g in range(GROUPS)]
        s_in = [inputs.tile([P, PACK, D], BF16, name="s_in%d" % g) for g in range(GROUPS)]

        def load_slices(dst, src, g, count):
            for t in range(0, PACK, count):
                nc.sync.dma_start(
                    out=dst[g][:, t : t + count, :], in_=src[g][:, t : t + count, :]
                )

        for part in (slice(0, D // 2), slice(D // 2, D)):
            nc.sync.dma_start(out=w_in[:, 0, part], in_=w_view[:, 0, part])
        for c in range(1, CHUNKS):
            nc.sync.dma_start(out=w_in[:, c, :], in_=w_view[:, c, :])
        for g in range(GROUPS):
            count = 1 if g < 2 else 2
            load_slices(h_in, h_view, g, count)
            load_slices(s_in, s_view, g, count)

        bias_all = const.tile([P, F], BF16, name="bias_all")
        gate_consts = const.tile([P, CONST_COLS], F32, name="gate_consts")
        w_grouped = keep.tile([P, CHUNKS * WORDS * PACK], BF16, name="w_grouped", align_bytes=64)
        w_words = keep.tile([P, CHUNKS * WORDS], U32, name="w_words", align_bytes=64)
        w_scales = keep.tile([P, CHUNKS * WORDS], U8, name="w_scales", align_bytes=64)

        flipped = {}
        h_grouped, h_words, h_scales = {}, {}, {}
        pre_banks = {}
        biased, weighted, weighted_words, weighted_scales = {}, {}, {}, {}
        square_sums, magnitudes, gates = {}, {}, {}
        gram_banks = {}

        def transpose_pairs(key, rows, index):
            pairs = rows.bitcast(F32)
            planes = bank(index, [P, 2 * PASSES, P], "flipped")
            for j in range(2 * PASSES):
                nc.tensor.transpose(planes[:, j, :], pairs[:, j * P : (j + 1) * P], identity[:])
            flipped[key] = planes

        def copy_out(key, grouped, on_vector):
            pairs = grouped.bitcast(F32).rearrange("p (k r u) -> p k r u", k=PASSES, r=P, u=2)
            alternating = flipped[key][:].rearrange("p (k u) r -> p k r u", u=2)
            if on_vector:
                nc.vector.tensor_copy(out=pairs, in_=alternating)
            else:
                nc.scalar.copy(out=pairs, in_=alternating)

        def copy_w(c, on_vector):
            copy_out(("w", c), w_grouped[:, c * WORDS * PACK : (c + 1) * WORDS * PACK], on_vector)

        def quantise_w(first):
            words = slice(first * WORDS, (first + 2) * WORDS)
            nc.vector.quantize_mx(
                out=w_words[:, words].bitcast(FP8X4), scales=w_scales[:, words],
                in_=w_grouped[:, first * WORDS * PACK : (first + 2) * WORDS * PACK],
            )

        def copy_h(g, t, on_vector):
            if g not in h_grouped:
                h_grouped[g] = rotate.tile(
                    [P, PACK * WORDS * PACK], BF16, name="h_grouped", align_bytes=64
                )
            copy_out((g, t), h_grouped[g][:, t * WORDS * PACK : (t + 1) * WORDS * PACK], on_vector)

        def quantise_h(g, first):
            if g not in h_words:
                h_words[g] = rotate.tile([P, PACK * WORDS], U32, name="h_words", align_bytes=64)
                h_scales[g] = rotate.tile([P, PACK * WORDS], U8, name="h_scales", align_bytes=64)
            words = slice(first * WORDS, (first + 2) * WORDS)
            nc.vector.quantize_mx(
                out=h_words[g][:, words].bitcast(FP8X4), scales=h_scales[g][:, words],
                in_=h_grouped[g][:, first * WORDS * PACK : (first + 2) * WORDS * PACK],
            )

        def project(g, first):
            for c in range(CHUNKS):
                if (g, c) not in pre_banks:
                    pre_banks[(g, c)] = bank(c, [P, PACK, P], "pre")
                for t in (first, first + 1):
                    for k in range(PASSES):
                        tokens = slice(t * WORDS + k * P, t * WORDS + (k + 1) * P)
                        features = slice(c * WORDS + k * P, c * WORDS + (k + 1) * P)
                        nc.tensor.matmul_mx(
                            out=pre_banks[(g, c)][:, t, :],
                            lhsT=h_words[g][:, tokens].bitcast(FP8X4),
                            lhsT_scale=h_scales[g][:, tokens],
                            rhs=w_words[:, features].bitcast(FP8X4),
                            rhs_scale=w_scales[:, features],
                            start=(k == 0),
                            stop=(k == PASSES - 1),
                        )

        def add_bias(g, c):
            if g not in biased:
                biased[g] = rotate.tile([P, F, PACK], F32, name="biased")
            features = slice(c * P, (c + 1) * P)
            nc.vector.tensor_tensor(
                out=biased[g][:, features, :],
                in0=pre_banks[(g, c)][:].rearrange("p t f -> p f t"),
                in1=bias_all[:, features].unsqueeze(2).to_broadcast([P, P, PACK]),
                op=ALU.add,
            )

        def sum_squares(g, t, on_vector=False):
            if g not in square_sums:
                square_sums[g] = keep.tile([P, PACK], F32, name="square_sums%d" % g)
            rows, total = s_in[g][:, t, :], square_sums[g][:, t : t + 1]
            if on_vector:
                unused = rotate.tile([P, D], BF16, name="unused_v")
                nc.vector.scalar_tensor_tensor(
                    out=unused[:], in0=rows, scalar=1.0, in1=rows, op0=ALU.mult, op1=ALU.mult,
                    accum_out=total,
                )
            else:
                unused = rotate.tile([P, D], BF16, name="unused_s")
                nc.scalar.activation(out=unused[:], in_=rows, func=ACT.Square, accum_out=total)

        def root_of_sums(g):
            magnitudes[g] = keep.tile([P, PACK], F32, name="magnitudes%d" % g)
            nc.gpsimd.tensor_tensor(
                out=magnitudes[g][:], in0=square_sums[g][:], in1=half[:], op=ALU.pow
            )

        def root_part(g, a, b):
            if g not in magnitudes:
                magnitudes[g] = keep.tile([P, PACK], F32, name="magnitudes%d" % g)
            nc.gpsimd.tensor_tensor(
                out=magnitudes[g][:, a:b], in0=square_sums[g][:, a:b], in1=half[:, a:b], op=ALU.pow
            )

        def make_gate(g):
            s = keep.tile([P, PACK], F32, name="s%d" % g)
            nc.scalar.activation(
                out=s[:], in_=magnitudes[g][:], func=ACT.Sigmoid,
                scale=gate_consts[:, GAIN_COL : GAIN_COL + 1],
                bias=gate_consts[:, BIAS_COL : BIAS_COL + 1],
            )
            gates[g] = keep.tile([P, PACK], F32, name="gates%d" % g)
            nc.gpsimd.tensor_tensor(out=gates[g][:], in0=s[:], in1=half[:], op=ALU.pow)

        def apply_gate(g, first, last):
            if g not in weighted:
                weighted[g] = rotate.tile([P, F, PACK], BF16, name="weighted", align_bytes=64)
            features = slice(first * P, last * P)
            nc.vector.tensor_tensor(
                out=weighted[g][:, features, :], in0=biased[g][:, features, :],
                in1=gates[g][:].unsqueeze(1).to_broadcast([P, (last - first) * P, PACK]),
                op=ALU.mult,
            )

        def apply_gate_on_scalar(g, c):
            features = slice(c * P, (c + 1) * P)
            for t in range(PACK):
                nc.scalar.activation(
                    out=weighted[g][:, features, t], in_=biased[g][:, features, t], func=ACT.Copy,
                    scale=gates[g][:, t : t + 1],
                )

        def quantise_weighted(g, first, last):
            if g not in weighted_words:
                weighted_words[g] = keep.tile([P, F], U32, name="weighted_words%d" % g, align_bytes=64)
                weighted_scales[g] = keep.tile([P, F], U8, name="weighted_scales%d" % g, align_bytes=64)
            features = slice(first * P, last * P)
            nc.vector.quantize_mx(
                out=weighted_words[g][:, features].bitcast(FP8X4),
                scales=weighted_scales[g][:, features],
                in_=weighted[g][:, features, :].rearrange("p f t -> p (f t)"),
            )

        def gram_pass(g, m, sums, cols):
            rows = slice(m * P, (m + 1) * P)
            nc.tensor.matmul_mx(
                out=sums,
                lhsT=weighted_words[g][:, rows].bitcast(FP8X4),
                lhsT_scale=weighted_scales[g][:, rows],
                rhs=weighted_words[g][:, cols].bitcast(FP8X4),
                rhs_scale=weighted_scales[g][:, cols],
                start=(g % 2 == 0),
                stop=(g % 2 == 1),
            )

        def gram_first_sample(g):
            for m in range(CHUNKS):
                if g == 0:
                    gram_banks[m] = bank(upper + m, [P, F], "gram")
                gram_pass(g, m, gram_banks[m][:], slice(0, F))

        def gram_second_sample(g):
            for h in range(2):
                for m in range(CHUNKS):
                    if g == 2:
                        gram_banks[(m, h)] = bank(upper + m if h == 0 else m, [P, HALF], "gram_half")
                    gram_pass(g, m, gram_banks[(m, h)][:], slice(h * HALF, (h + 1) * HALF))

        def store(sample, m, cols, sums, pool, name, on_vector):
            scaled = pool.tile([P, cols.stop - cols.start], F32, name=name)
            if on_vector:
                nc.vector.tensor_scalar_mul(out=scaled[:], in0=sums[:], scalar1=1.0 / TOKENS)
            else:
                nc.scalar.mul(out=scaled[:], in_=sums[:], mul=1.0 / TOKENS)
            nc.sync.dma_start(out=out[sample, m * P : (m + 1) * P, cols], in_=scaled[:])

        for c in range(CHUNKS):
            transpose_pairs(("w", c), w_in[:, c, :], c)
        for t in range(PACK):
            transpose_pairs((0, t), h_in[0][:, t, :], upper + t)
        copy_w(0, True)
        copy_w(1, False)
        copy_w(2, True)
        copy_w(3, False)
        quantise_w(0)
        copy_h(0, 0, True)
        quantise_w(2)
        for t in range(1, PACK):
            copy_h(0, t, False)
        spread = bank(upper, [P, F], "spread", BF16)
        nc.tensor.matmul(out=spread[:], lhsT=ones[:], rhs=const_row[:, 0:F], start=True, stop=True)
        spread_consts = bank(upper + 1, [P, CONST_COLS], "spread_consts")
        nc.tensor.matmul(
            out=spread_consts[:], lhsT=ones[:], rhs=const_row[:, F : F + CONST_COLS],
            start=True, stop=True,
        )
        quantise_h(0, 0)
        nc.vector.tensor_copy(out=bias_all[:], in_=spread[:])
        quantise_h(0, 2)
        nc.vector.tensor_copy(out=gate_consts[:], in_=spread_consts[:])
        project(0, 0)
        project(0, 2)
        sum_squares(0, 0, on_vector=True)
        for t in range(1, PACK):
            sum_squares(0, t)
        root_of_sums(0)

        for r in range(GROUPS):
            ahead = r + 1
            if r < 2:
                for t in range(PACK):
                    transpose_pairs((ahead, t), h_in[ahead][:, t, :], upper + t)
            for c in range(CHUNKS):
                add_bias(r, c)
                if r == 2:
                    transpose_pairs((ahead, c), h_in[ahead][:, c, :], c)
            if ahead < GROUPS:
                on_vector = (0, 3) if r == 0 else (0,)
                on_scalar = [t for t in range(PACK) if t not in on_vector]
                if r == 0:
                    for t in on_scalar:
                        copy_h(ahead, t, False)
                    make_gate(r)
                    sum_squares(ahead, 0)
                else:
                    sum_squares(ahead, 0)
                    make_gate(r)
                    for t in on_scalar:
                        copy_h(ahead, t, False)
                for t in range(1, PACK):
                    sum_squares(ahead, t)
                    if ahead == 3 and t == 2:
                        root_part(ahead, 0, 3)
                if ahead == 3:
                    root_part(ahead, 3, 4)
                else:
                    root_of_sums(ahead)
                for t in on_vector:
                    copy_h(ahead, t, True)
            else:
                for m in range(CHUNKS):
                    if m == 2:
                        make_gate(r)
                    store(0, m, slice(0, F), gram_banks[m], results, "scaled", False)
            if r >= 1:
                quantise_weighted(r - 1, 0, CHUNKS)
                if r < GROUPS - 1:
                    gram_first_sample(r - 1)
                else:
                    gram_second_sample(r - 1)
            if ahead < GROUPS:
                for first in (0, 2):
                    quantise_h(ahead, first)
                    project(ahead, first)
                apply_gate(r, 0, CHUNKS)
        last = GROUPS - 1
        apply_gate(last, 0, 2)
        apply_gate(last, 2, 3)
        apply_gate_on_scalar(last, 3)
        quantise_weighted(last, 0, 2)
        quantise_weighted(last, 2, 4)
        gram_second_sample(last)
        for h in range(2):
            for m in range(CHUNKS):
                cols = slice(h * HALF, (h + 1) * HALF)
                store(1, m, cols, gram_banks[(m, h)], halves, "scaled_half", m % 2 == 1)
